import numpy as np
import ml_dtypes


def mxq(x, axis, fmt="e4m3"):
    dtype, down = {"e4m3": (ml_dtypes.float8_e4m3fn, 7), "e5m2": (ml_dtypes.float8_e5m2, 14)}[fmt]
    v = np.moveaxis(np.asarray(x, np.float32).astype(ml_dtypes.bfloat16).astype(np.float64), axis, -1)
    blocks = v.reshape(v.shape[:-1] + (-1, 32))
    amax = np.abs(blocks).max(-1, keepdims=True)
    byte = np.maximum(np.where(amax > 0, np.frexp(amax)[1] - 1 + 127, 0) - down, 1)
    scale = np.exp2(byte - 127.0)
    codes = (blocks / scale).astype(np.float32).astype(dtype).astype(np.float64)
    return np.moveaxis((codes * scale).reshape(v.shape), -1, axis)


WIDE = False


def mx_kscale(k):
    if not WIDE:
        return np.ones(k)
    levels = np.array([10, -10, 5, -5, 0])
    if k % 512:
        return np.exp2(np.random.permutation(np.resize(levels, k // 32))).repeat(32)
    a = np.empty((k // 512, 16))
    for p in range(k // 512):
        a[p, :8] = np.random.permutation(np.resize(levels, 8))
        for g in range(8):
            far = levels[np.abs(levels - a[p, g]) >= 10]
            a[p, g + 8] = far[np.random.randint(len(far))]
    return np.exp2(a.ravel()).repeat(32)


BF16 = ml_dtypes.bfloat16


def bf(x):
    return np.asarray(x, np.float32).astype(BF16)


def f64(x):
    return np.asarray(x).astype(np.float64)


E2M1 = np.array([0.0, 0.5, 1.0, 1.5, 2.0, 3.0, 4.0, 6.0, -0.0, -0.5, -1.0, -1.5, -2.0, -3.0, -4.0, -6.0])


def pack_weight(w, fmt):
    k, n = w.shape
    w = f64(bf(w)).reshape(k // 32, 32, n)
    amax = np.abs(w).max(1)
    if fmt == "e4m3":
        byte = np.frexp(amax)[1] - 1 + 127 - 7
    else:
        mant, ex = np.frexp(amax / 6.0)
        byte = np.where(mant > 0.5, ex, ex - 1) + 127
    byte = np.clip(np.where(amax > 0, byte, 1), 1, 254)
    scaled = (w * np.exp2(127.0 - byte)[:, None, :]).reshape(k, n).astype(np.float32)
    by_word = np.ascontiguousarray(scaled.reshape(k // 512, 128, 4, n).transpose(0, 1, 3, 2))
    if fmt == "e4m3":
        words = by_word.astype(ml_dtypes.float8_e4m3fn).view(np.uint8)
    else:
        c = by_word.astype(ml_dtypes.float4_e2m1fn).view(np.uint8) & 0xF
        words = c[..., 0::2] | (c[..., 1::2] << 4)
    return np.ascontiguousarray(words), np.ascontiguousarray(byte.astype(np.uint8).reshape(k // 512, 16, n))


def unpack_weight(words, scales, fmt):
    g, p, n, _ = words.shape
    if fmt == "e4m3":
        vals = np.ascontiguousarray(words).view(ml_dtypes.float8_e4m3fn).astype(np.float64)
    else:
        nib = np.empty((g, p, n, 4), np.uint8)
        nib[..., 0::2] = words & 0xF
        nib[..., 1::2] = words >> 4
        vals = E2M1[nib]
    vals = vals * np.repeat(np.exp2(scales.astype(np.float64) - 127.0), 8, axis=1)[..., None]
    return vals.transpose(0, 1, 3, 2).reshape(g * 512, n)


BS, N, D, B, D_PM = 2, 1024, 1024, 8, 512


def setup_inputs():
    k, t = mx_kscale(D_PM), mx_kscale(D_PM)
    w = np.eye(D_PM) / B + 1.6 / np.sqrt(B * D_PM) * np.random.standard_normal((BS, B, D_PM, D_PM))
    pre = bf(np.random.standard_normal((BS, N, D_PM)) * k)
    W_pm = bf(w * t[:, None] / k)
    proj = np.random.standard_normal((D, D_PM)) / np.sqrt(D_PM) / t
    words, scales = pack_weight(proj.T, "e4m3")
    proj_out_b = bf(np.random.standard_normal(D) * 0.3)
    return {"pre": pre,
            "W_pm": W_pm,
            "proj_out_w_words": words,
            "proj_out_w_scales": scales,
            "proj_out_b": proj_out_b}


def reference(pre, W_pm, proj_out_w_words, proj_out_w_scales, proj_out_b):
    W_sum = np.sum(f64(W_pm), axis=1)
    post = mxq(f64(pre), 2, "e4m3") @ mxq(W_sum, 2, "e4m3").transpose(0, 2, 1)
    return (mxq(post, 2, "e4m3") @ unpack_weight(proj_out_w_words, proj_out_w_scales, "e4m3")) + f64(proj_out_b)

@@ -1,0 +1,267 @@
+from contextlib import ExitStack
+
+import concourse.mybir as mybir
+from concourse.masks import make_identity
+
+FLOPS = 2 * 2 * 1024 * 512 * 512 + 2 * 2 * 1024 * 512 * 1024
+
+FP8X4 = mybir.dt.float8_e4m3fn_x4
+BF16 = mybir.dt.bfloat16
+F32 = mybir.dt.float32
+I32 = mybir.dt.int32
+U32 = mybir.dt.uint32
+U8 = mybir.dt.uint8
+ADD = mybir.AluOpType.add
+
+P = 128
+PACK = 4
+SAMPLES = 2
+TOKENS = 1024
+MEM = 512
+FEAT = 1024
+BANKS = 8
+BLOCKS = TOKENS // P
+HALF = 512
+ROW_GROUPS = P // BANKS
+ROWS = MEM // ROW_GROUPS
+CHUNK_ROWS = 8
+CHUNKS = ROWS // CHUNK_ROWS
+HALF_BLOCKS = BLOCKS // 2
+
+
+def tile_proceduralmemory_pc_kernel(
+    tc, pre, W_pm, proj_out_w_words, proj_out_w_scales, proj_out_b, out
+):
+    nc = tc.nc
+    with ExitStack() as ctx:
+        ctx.enter_context(tc.manual_schedule())
+        consts = ctx.enter_context(tc.tile_pool(name="consts", bufs=1))
+        sample = ctx.enter_context(tc.tile_pool(name="sample", bufs=SAMPLES))
+        halves = ctx.enter_context(tc.tile_pool(name="halves", bufs=2 * SAMPLES))
+        banks = ctx.enter_context(tc.tile_pool(name="banks", bufs=SAMPLES * CHUNKS))
+        work = ctx.enter_context(tc.tile_pool(name="work", bufs=4))
+        results = ctx.enter_context(tc.tile_pool(name="results", bufs=SAMPLES * BLOCKS))
+        psum_early = ctx.enter_context(tc.psum_pool(name="psum_early", bufs=2))
+        psum_post = ctx.enter_context(tc.psum_pool(name="psum_post", bufs=2))
+        psum_product = ctx.enter_context(tc.psum_pool(name="psum_product", bufs=4))
+
+        ones = consts.tile([P, P], BF16)
+        nc.vector.memset(ones[:], 1.0)
+        bias_row = consts.tile([P, FEAT], BF16)
+        nc.vector.memset(bias_row[:], 0.0)
+        bias_all = consts.tile([P, FEAT], F32)
+        w_words = consts.tile([P, FEAT], U32, align_bytes=64)
+        w_scales = consts.tile([P, FEAT], U8, align_bytes=64)
+        nc.vector.memset(w_scales[:].bitcast(I32), 0)
+        ident = consts.tile([P, P], BF16)
+        make_identity(nc, ident[:])
+        fold_f32 = consts.tile([P, ROW_GROUPS], F32)
+        nc.vector.tensor_reduce(
+            out=fold_f32[:],
+            in_=ident[:].rearrange("q (k r) -> q r k", r=ROW_GROUPS),
+            axis=mybir.AxisListType.X,
+            op=ADD,
+        )
+        fold = consts.tile([P, ROW_GROUPS], BF16)
+        nc.vector.tensor_copy(out=fold[:], in_=fold_f32[:])
+
+        pre_rows = {}
+        bank_rows = {}
+
+        def load_tokens(b):
+            tokens_view = pre[b].rearrange("(p nb) j -> p nb j", nb=BLOCKS)
+            for half in range(2):
+                pre_tile = halves.tile([P, HALF_BLOCKS, MEM], BF16)
+                nc.sync.dma_start(
+                    out=pre_tile[:],
+                    in_=tokens_view[:, half * HALF_BLOCKS : (half + 1) * HALF_BLOCKS, :],
+                )
+                pre_rows[(b, half)] = pre_tile
+
+        def load_banks(b):
+            rows_view = W_pm[b].rearrange("k (r s) j -> (k r) s j", s=ROWS)
+            for c in range(CHUNKS):
+                chunk_tile = banks.tile([P, CHUNK_ROWS, MEM], BF16)
+                nc.sync.dma_start(
+                    out=chunk_tile[:],
+                    in_=rows_view[:, c * CHUNK_ROWS : (c + 1) * CHUNK_ROWS, :],
+                )
+                bank_rows[(b, c)] = chunk_tile
+
+        load_tokens(0)
+        nc.sync.dma_start(
+            out=bias_row[0:1, :], in_=proj_out_b.rearrange("(o d) -> o d", o=1)
+        )
+        load_banks(0)
+        nc.sync.dma_start(
+            out=w_words[:].bitcast(I32),
+            in_=proj_out_w_words[0].rearrange("p n t -> p (n t)").bitcast(I32),
+        )
+        for quadrant in range(4):
+            nc.sync.dma_start(
+                out=w_scales[32 * quadrant : 32 * quadrant + 4, :].bitcast(I32),
+                in_=proj_out_w_scales[0, 4 * quadrant : 4 * quadrant + 4, :].bitcast(I32),
+            )
+        load_tokens(1)
+        load_banks(1)
+
+        pre_codes = {}
+        pre_scales = {}
+        wsum_grouped = {}
+        wsum_codes = {}
+        wsum_scales = {}
+        for b in range(SAMPLES):
+            codes = sample.tile([P, TOKENS], U32, align_bytes=64)
+            scales = sample.tile([P, TOKENS], U8, align_bytes=64)
+            grouped_sums = sample.tile(
+                [P, PACK, ROW_GROUPS, ROWS // PACK, PACK], BF16, align_bytes=64
+            )
+            codes_w = sample.tile([P, MEM], U32, align_bytes=64)
+            scales_w = sample.tile([P, MEM], U8, align_bytes=64)
+            pre_codes[b] = codes
+            pre_scales[b] = scales
+            wsum_grouped[b] = grouped_sums
+            wsum_codes[b] = codes_w
+            wsum_scales[b] = scales_w
+
+        def quantise_tokens(b, half):
+            grouped = halves.tile([P, HALF_BLOCKS, P, PACK], BF16, align_bytes=64)
+            for nb in range(HALF_BLOCKS):
+                flipped = psum_early.tile([P, PACK, P], BF16, tag="early")
+                for t in range(PACK):
+                    nc.tensor.transpose(
+                        out=flipped[:, t, :],
+                        in_=pre_rows[(b, half)][:, nb, t:MEM:PACK],
+                        identity=ident[:],
+                    )
+                copy = nc.scalar.copy if nb % 2 == 0 else nc.vector.tensor_copy
+                copy(out=grouped[:, nb, :, :], in_=flipped[:].rearrange("p t n -> p n t"))
+            cols = slice(half * HALF_BLOCKS * P, (half + 1) * HALF_BLOCKS * P)
+            nc.vector.quantize_mx(
+                out=pre_codes[b][:, cols].bitcast(FP8X4),
+                scales=pre_scales[b][:, cols],
+                in_=grouped[:].rearrange("p nb n t -> p (nb n t)"),
+            )
+
+        def sum_banks(b, c):
+            sums = psum_early.tile(
+                [P, PACK, ROW_GROUPS, CHUNK_ROWS // PACK, PACK], F32, tag="early"
+            )
+            for s in range(CHUNK_ROWS):
+                for t in range(PACK):
+                    nc.tensor.matmul(
+                        out=sums[:, s % PACK, :, s // PACK, t],
+                        lhsT=bank_rows[(b, c)][:, s, t:MEM:PACK],
+                        rhs=fold[:],
+                        start=True,
+                        stop=True,
+                    )
+            per_chunk = CHUNK_ROWS // PACK
+            nc.scalar.copy(
+                out=wsum_grouped[b][:].rearrange("p T r s t -> p (T r) s t")[
+                    :, :, c * per_chunk : (c + 1) * per_chunk, :
+                ],
+                in_=sums[:].rearrange("p T r s t -> p (T r) s t"),
+            )
+
+        def quantise_bank_sums(b):
+            nc.vector.quantize_mx(
+                out=wsum_codes[b][:].bitcast(FP8X4),
+                scales=wsum_scales[b][:],
+                in_=wsum_grouped[b][:].rearrange("p T r s t -> p (T r s t)"),
+            )
+
+        def spread_bias():
+            for h in range(FEAT // HALF):
+                cols = slice(h * HALF, (h + 1) * HALF)
+                product = psum_product.tile([P, HALF], F32)
+                nc.tensor.matmul(
+                    out=product[:], lhsT=ones[:], rhs=bias_row[:, cols], start=True, stop=True
+                )
+                nc.scalar.copy(out=bias_all[:, cols], in_=product[:])
+
+        post_grouped = {}
+        post_codes = {}
+        post_scales = {}
+        products = {}
+
+        def first_product(g):
+            b, nb = divmod(g, BLOCKS)
+            post = psum_post.tile([P, PACK, P], F32)
+            tokens = slice(nb * P, (nb + 1) * P)
+            for T in range(PACK):
+                rows = slice(T * P, (T + 1) * P)
+                nc.tensor.matmul_mx(
+                    out=post[:, T, :],
+                    lhsT=wsum_codes[b][:, rows].bitcast(FP8X4),
+                    lhsT_scale=wsum_scales[b][:, rows],
+                    rhs=pre_codes[b][:, tokens].bitcast(FP8X4),
+                    rhs_scale=pre_scales[b][:, tokens],
+                    start=True,
+                    stop=True,
+                )
+            grouped_post = work.tile([P, P, PACK], BF16, align_bytes=64)
+            nc.scalar.copy(out=grouped_post[:], in_=post[:].rearrange("p T n -> p n T"))
+            post_grouped[g] = grouped_post
+
+        def quantise_post(g):
+            codes_p = work.tile([P, P], U32, align_bytes=64)
+            scales_p = work.tile([P, P], U8, align_bytes=64)
+            nc.vector.quantize_mx(
+                out=codes_p[:].bitcast(FP8X4),
+                scales=scales_p[:],
+                in_=post_grouped[g][:].rearrange("p n T -> p (n T)"),
+            )
+            post_codes[g] = codes_p
+            post_scales[g] = scales_p
+
+        def second_product(g):
+            for h in range(FEAT // HALF):
+                cols = slice(h * HALF, (h + 1) * HALF)
+                product = psum_product.tile([P, HALF], F32)
+                nc.tensor.matmul_mx(
+                    out=product[:],
+                    lhsT=post_codes[g][:].bitcast(FP8X4),
+                    lhsT_scale=post_scales[g][:],
+                    rhs=w_words[:, cols].bitcast(FP8X4),
+                    rhs_scale=w_scales[:, cols],
+                    start=True,
+                    stop=True,
+                )
+                products[(g, h)] = product
+
+        def add_bias_and_store(g):
+            b, nb = divmod(g, BLOCKS)
+            result = results.tile([P, FEAT], F32)
+            for h in range(FEAT // HALF):
+                cols = slice(h * HALF, (h + 1) * HALF)
+                nc.vector.tensor_tensor(
+                    out=result[:, cols], in0=products[(g, h)][:], in1=bias_all[:, cols], op=ADD
+                )
+            nc.sync.dma_start(
+                out=out[b].rearrange("(p nb) d -> p nb d", nb=BLOCKS)[:, nb, :], in_=result[:]
+            )
+
+        quantise_tokens(0, 0)
+        quantise_tokens(0, 1)
+        for c in range(CHUNKS):
+            sum_banks(0, c)
+        quantise_bank_sums(0)
+        spread_bias()
+
+        n_blocks = SAMPLES * BLOCKS
+        for step in range(-2, n_blocks):
+            if step + 2 < n_blocks:
+                first_product(step + 2)
+            if 0 <= step + 1 < n_blocks:
+                second_product(step + 1)
+            if step >= 0:
+                add_bias_and_store(step)
+            if step + 2 < n_blocks:
+                quantise_post(step + 2)
+            if step < 0:
+                quantise_tokens(1, step + 2)
+            elif step < CHUNKS:
+                sum_banks(1, step)
+            elif step == CHUNKS:
+                quantise_bank_sums(1)

@@ -26,7 +26,12 @@ ROW_GROUPS = P // BANKS
 ROWS = MEM // ROW_GROUPS
 CHUNK_ROWS = 8
 CHUNKS = ROWS // CHUNK_ROWS
+PER_CHUNK = CHUNK_ROWS // PACK
+T_HALF = PACK // 2
 HALF_BLOCKS = BLOCKS // 2
+PAIR = 2
+WORDS = MEM // 2
+WORD_PACK = PACK // 2
 
 
 def tile_proceduralmemory_pc_kernel(
@@ -41,10 +46,12 @@ def tile_proceduralmemory_pc_kernel(
         banks = ctx.enter_context(tc.tile_pool(name="banks", bufs=SAMPLES * CHUNKS))
         work = ctx.enter_context(tc.tile_pool(name="work", bufs=4))
         results = ctx.enter_context(tc.tile_pool(name="results", bufs=SAMPLES * BLOCKS))
-        psum_early = ctx.enter_context(tc.psum_pool(name="psum_early", bufs=2))
+        psum_sums = ctx.enter_context(tc.psum_pool(name="psum_sums", bufs=2))
         psum_post = ctx.enter_context(tc.psum_pool(name="psum_post", bufs=2))
         psum_product = ctx.enter_context(tc.psum_pool(name="psum_product", bufs=4))
 
+        ident = consts.tile([P, P], F32)
+        make_identity(nc, ident[:])
         ones = consts.tile([P, P], BF16)
         nc.vector.memset(ones[:], 1.0)
         bias_row = consts.tile([P, FEAT], BF16)
@@ -53,8 +60,6 @@ def tile_proceduralmemory_pc_kernel(
         w_words = consts.tile([P, FEAT], U32, align_bytes=64)
         w_scales = consts.tile([P, FEAT], U8, align_bytes=64)
         nc.vector.memset(w_scales[:].bitcast(I32), 0)
-        ident = consts.tile([P, P], BF16)
-        make_identity(nc, ident[:])
         fold_f32 = consts.tile([P, ROW_GROUPS], F32)
         nc.vector.tensor_reduce(
             out=fold_f32[:],
@@ -68,15 +73,14 @@ def tile_proceduralmemory_pc_kernel(
         pre_rows = {}
         bank_rows = {}
 
-        def load_tokens(b):
+        def load_tokens(b, half):
             tokens_view = pre[b].rearrange("(p nb) j -> p nb j", nb=BLOCKS)
-            for half in range(2):
-                pre_tile = halves.tile([P, HALF_BLOCKS, MEM], BF16)
-                nc.sync.dma_start(
-                    out=pre_tile[:],
-                    in_=tokens_view[:, half * HALF_BLOCKS : (half + 1) * HALF_BLOCKS, :],
-                )
-                pre_rows[(b, half)] = pre_tile
+            pre_tile = halves.tile([P, HALF_BLOCKS, MEM], BF16)
+            nc.sync.dma_start(
+                out=pre_tile[:],
+                in_=tokens_view[:, half * HALF_BLOCKS : (half + 1) * HALF_BLOCKS, :],
+            )
+            pre_rows[(b, half)] = pre_tile
 
         def load_banks(b):
             rows_view = W_pm[b].rearrange("k (r s) j -> (k r) s j", s=ROWS)
@@ -88,21 +92,29 @@ def tile_proceduralmemory_pc_kernel(
                 )
                 bank_rows[(b, c)] = chunk_tile
 
-        load_tokens(0)
-        nc.sync.dma_start(
-            out=bias_row[0:1, :], in_=proj_out_b.rearrange("(o d) -> o d", o=1)
-        )
-        load_banks(0)
-        nc.sync.dma_start(
-            out=w_words[:].bitcast(I32),
-            in_=proj_out_w_words[0].rearrange("p n t -> p (n t)").bitcast(I32),
-        )
-        for quadrant in range(4):
+        def load_bias():
             nc.sync.dma_start(
-                out=w_scales[32 * quadrant : 32 * quadrant + 4, :].bitcast(I32),
-                in_=proj_out_w_scales[0, 4 * quadrant : 4 * quadrant + 4, :].bitcast(I32),
+                out=bias_row[0:1, :], in_=proj_out_b.rearrange("(o d) -> o d", o=1)
             )
-        load_tokens(1)
+
+        def load_projection():
+            nc.sync.dma_start(
+                out=w_words[:].bitcast(I32),
+                in_=proj_out_w_words[0].rearrange("p n t -> p (n t)").bitcast(I32),
+            )
+            for quadrant in range(4):
+                nc.sync.dma_start(
+                    out=w_scales[32 * quadrant : 32 * quadrant + 4, :].bitcast(I32),
+                    in_=proj_out_w_scales[0, 4 * quadrant : 4 * quadrant + 4, :].bitcast(I32),
+                )
+
+        load_tokens(0, 0)
+        load_tokens(0, 1)
+        load_bias()
+        load_tokens(1, 0)
+        load_tokens(1, 1)
+        load_banks(0)
+        load_projection()
         load_banks(1)
 
         pre_codes = {}
@@ -125,17 +137,29 @@ def tile_proceduralmemory_pc_kernel(
             wsum_scales[b] = scales_w
 
         def quantise_tokens(b, half):
+            words = pre_rows[(b, half)][:].rearrange("p nb j -> p (nb j)").bitcast(F32)
             grouped = halves.tile([P, HALF_BLOCKS, P, PACK], BF16, align_bytes=64)
-            for nb in range(HALF_BLOCKS):
-                flipped = psum_early.tile([P, PACK, P], BF16, tag="early")
-                for t in range(PACK):
-                    nc.tensor.transpose(
-                        out=flipped[:, t, :],
-                        in_=pre_rows[(b, half)][:, nb, t:MEM:PACK],
-                        identity=ident[:],
-                    )
-                copy = nc.scalar.copy if nb % 2 == 0 else nc.vector.tensor_copy
-                copy(out=grouped[:, nb, :, :], in_=flipped[:].rearrange("p t n -> p n t"))
+            grouped_words = (
+                grouped[:]
+                .rearrange("p nb n t -> p (nb n t)")
+                .bitcast(F32)
+                .rearrange("p (nb n u) -> p nb n u", nb=HALF_BLOCKS, u=WORD_PACK)
+            )
+            for pair in range(HALF_BLOCKS // PAIR):
+                flipped = psum_product.tile([P, PAIR, WORD_PACK, P], F32, tag="product")
+                for k in range(PAIR):
+                    row = (pair * PAIR + k) * WORDS
+                    for u in range(WORD_PACK):
+                        nc.tensor.transpose(
+                            out=flipped[:, k, u, :],
+                            in_=words[:, row + u : row + WORDS : WORD_PACK],
+                            identity=ident[:],
+                        )
+                copy = nc.scalar.copy if pair % 2 == 0 else nc.vector.tensor_copy
+                copy(
+                    out=grouped_words[:, pair * PAIR : (pair + 1) * PAIR, :, :],
+                    in_=flipped[:].rearrange("p k u n -> p k n u"),
+                )
             cols = slice(half * HALF_BLOCKS * P, (half + 1) * HALF_BLOCKS * P)
             nc.vector.quantize_mx(
                 out=pre_codes[b][:, cols].bitcast(FP8X4),
@@ -143,42 +167,44 @@ def tile_proceduralmemory_pc_kernel(
                 in_=grouped[:].rearrange("p nb n t -> p (nb n t)"),
             )
 
-        def sum_banks(b, c):
-            sums = psum_early.tile(
-                [P, PACK, ROW_GROUPS, CHUNK_ROWS // PACK, PACK], F32, tag="early"
-            )
-            for s in range(CHUNK_ROWS):
-                for t in range(PACK):
-                    nc.tensor.matmul(
-                        out=sums[:, s % PACK, :, s // PACK, t],
-                        lhsT=bank_rows[(b, c)][:, s, t:MEM:PACK],
-                        rhs=fold[:],
-                        start=True,
-                        stop=True,
-                    )
-            per_chunk = CHUNK_ROWS // PACK
+        def sum_banks(b, c, h):
+            sums = psum_sums.tile([P, T_HALF, ROW_GROUPS, PER_CHUNK, PACK], F32)
+            for k in range(T_HALF):
+                for s1 in range(PER_CHUNK):
+                    s = PACK * s1 + T_HALF * h + k
+                    for t in range(PACK):
+                        nc.tensor.matmul(
+                            out=sums[:, k, :, s1, t],
+                            lhsT=bank_rows[(b, c)][:, s, t:MEM:PACK],
+                            rhs=fold[:],
+                            start=True,
+                            stop=True,
+                        )
             nc.scalar.copy(
-                out=wsum_grouped[b][:].rearrange("p T r s t -> p (T r) s t")[
-                    :, :, c * per_chunk : (c + 1) * per_chunk, :
-                ],
+                out=wsum_grouped[b][:, T_HALF * h : T_HALF * (h + 1)].rearrange(
+                    "p T r s t -> p (T r) s t"
+                )[:, :, c * PER_CHUNK : (c + 1) * PER_CHUNK, :],
                 in_=sums[:].rearrange("p T r s t -> p (T r) s t"),
             )
 
-        def quantise_bank_sums(b):
+        def quantise_bank_sums(b, h):
+            cols = slice(h * T_HALF * P, (h + 1) * T_HALF * P)
             nc.vector.quantize_mx(
-                out=wsum_codes[b][:].bitcast(FP8X4),
-                scales=wsum_scales[b][:],
-                in_=wsum_grouped[b][:].rearrange("p T r s t -> p (T r s t)"),
+                out=wsum_codes[b][:, cols].bitcast(FP8X4),
+                scales=wsum_scales[b][:, cols],
+                in_=wsum_grouped[b][:, T_HALF * h : T_HALF * (h + 1)].rearrange(
+                    "p T r s t -> p (T r s t)"
+                ),
             )
 
         def spread_bias():
             for h in range(FEAT // HALF):
                 cols = slice(h * HALF, (h + 1) * HALF)
-                product = psum_product.tile([P, HALF], F32)
+                spread = psum_post.tile([P, HALF], F32, tag="post")
                 nc.tensor.matmul(
-                    out=product[:], lhsT=ones[:], rhs=bias_row[:, cols], start=True, stop=True
+                    out=spread[:], lhsT=ones[:], rhs=bias_row[:, cols], start=True, stop=True
                 )
-                nc.scalar.copy(out=bias_all[:, cols], in_=product[:])
+                nc.scalar.copy(out=bias_all[:, cols], in_=spread[:])
 
         post_grouped = {}
         post_codes = {}
@@ -187,7 +213,7 @@ def tile_proceduralmemory_pc_kernel(
 
         def first_product(g):
             b, nb = divmod(g, BLOCKS)
-            post = psum_post.tile([P, PACK, P], F32)
+            post = psum_post.tile([P, PACK, P], F32, tag="post")
             tokens = slice(nb * P, (nb + 1) * P)
             for T in range(PACK):
                 rows = slice(T * P, (T + 1) * P)
@@ -218,7 +244,7 @@ def tile_proceduralmemory_pc_kernel(
         def second_product(g):
             for h in range(FEAT // HALF):
                 cols = slice(h * HALF, (h + 1) * HALF)
-                product = psum_product.tile([P, HALF], F32)
+                product = psum_product.tile([P, HALF], F32, tag="product")
                 nc.tensor.matmul_mx(
                     out=product[:],
                     lhsT=post_codes[g][:].bitcast(FP8X4),
@@ -244,11 +270,16 @@ def tile_proceduralmemory_pc_kernel(
 
         quantise_tokens(0, 0)
         quantise_tokens(0, 1)
-        for c in range(CHUNKS):
-            sum_banks(0, c)
-        quantise_bank_sums(0)
         spread_bias()
+        quantise_tokens(1, 0)
+        quantise_tokens(1, 1)
+        for c in range(CHUNKS):
+            for h in range(PACK // T_HALF):
+                sum_banks(0, c, h)
+                if c == CHUNKS - 1:
+                    quantise_bank_sums(0, h)
 
+        sums_at = {0: [0], 1: [1], 2: [2], 3: [3], 4: [4, 5], 5: [6, 7]}
         n_blocks = SAMPLES * BLOCKS
         for step in range(-2, n_blocks):
             if step + 2 < n_blocks:
@@ -259,9 +290,8 @@ def tile_proceduralmemory_pc_kernel(
                 add_bias_and_store(step)
             if step + 2 < n_blocks:
                 quantise_post(step + 2)
-            if step < 0:
-                quantise_tokens(1, step + 2)
-            elif step < CHUNKS:
-                sum_banks(1, step)
-            elif step == CHUNKS:
-                quantise_bank_sums(1)
+            for k in sums_at.get(step, []):
+                c, h = divmod(k, PACK // T_HALF)
+                sum_banks(1, c, h)
+                if c == CHUNKS - 1:
+                    quantise_bank_sums(1, h)

@@ -168,7 +168,7 @@ def tile_proceduralmemory_pc_kernel(
             )
 
         def sum_banks(b, c, h):
-            sums = psum_sums.tile([P, T_HALF, ROW_GROUPS, PER_CHUNK, PACK], F32)
+            sums = psum_sums.tile([P, T_HALF, ROW_GROUPS, PER_CHUNK, PACK], F32, tag="sums")
             for k in range(T_HALF):
                 for s1 in range(PER_CHUNK):
                     s = PACK * s1 + T_HALF * h + k
@@ -279,19 +279,20 @@ def tile_proceduralmemory_pc_kernel(
                 if c == CHUNKS - 1:
                     quantise_bank_sums(0, h)
 
-        sums_at = {0: [0], 1: [1], 2: [2], 3: [3], 4: [4, 5], 5: [6, 7]}
+        sums_at = {-1: [0], 0: [1], 1: [2], 2: [3], 3: [4, 5], 4: [6, 7]}
         n_blocks = SAMPLES * BLOCKS
-        for step in range(-2, n_blocks):
-            if step + 2 < n_blocks:
-                first_product(step + 2)
+        for step in range(-3, n_blocks):
             if 0 <= step + 1 < n_blocks:
                 second_product(step + 1)
             if step >= 0:
                 add_bias_and_store(step)
-            if step + 2 < n_blocks:
+            if 0 <= step + 2 < n_blocks:
                 quantise_post(step + 2)
             for k in sums_at.get(step, []):
                 c, h = divmod(k, PACK // T_HALF)
                 sum_banks(1, c, h)
-                if c == CHUNKS - 1:
+            if step + 3 == BLOCKS:
+                for h in range(PACK // T_HALF):
                     quantise_bank_sums(1, h)
+            if step + 3 < n_blocks:
+                first_product(step + 3)

@@ -23,6 +23,7 @@ BANKS = 8
 BLOCKS = TOKENS // P
 HALF = 512
 ROW_GROUPS = P // BANKS
+FOLD = 24
 ROWS = MEM // ROW_GROUPS
 CHUNK_ROWS = 8
 CHUNKS = ROWS // CHUNK_ROWS
@@ -57,6 +58,8 @@ def tile_proceduralmemory_pc_kernel(
         bias_row = consts.tile([P, FEAT], BF16)
         nc.vector.memset(bias_row[:], 0.0)
         bias_all = consts.tile([P, FEAT], F32)
+        zeros = consts.tile([P, HALF], BF16)
+        nc.vector.memset(zeros[:], 0.0)
         w_words = consts.tile([P, FEAT], U32, align_bytes=64)
         w_scales = consts.tile([P, FEAT], U8, align_bytes=64)
         nc.vector.memset(w_scales[:].bitcast(I32), 0)
@@ -67,8 +70,9 @@ def tile_proceduralmemory_pc_kernel(
             axis=mybir.AxisListType.X,
             op=ADD,
         )
-        fold = consts.tile([P, ROW_GROUPS], BF16)
-        nc.vector.tensor_copy(out=fold[:], in_=fold_f32[:])
+        fold = consts.tile([P, FOLD], BF16)
+        nc.vector.memset(fold[:], 0.0)
+        nc.vector.tensor_copy(out=fold[:, 0:ROW_GROUPS], in_=fold_f32[:])
 
         pre_rows = {}
         bank_rows = {}
@@ -168,7 +172,7 @@ def tile_proceduralmemory_pc_kernel(
             )
 
         def sum_banks(b, c, h):
-            sums = psum_sums.tile([P, T_HALF, ROW_GROUPS, PER_CHUNK, PACK], F32, tag="sums")
+            sums = psum_sums.tile([P, T_HALF, FOLD, PER_CHUNK, PACK], F32, tag="sums")
             for k in range(T_HALF):
                 for s1 in range(PER_CHUNK):
                     s = PACK * s1 + T_HALF * h + k
@@ -182,9 +186,9 @@ def tile_proceduralmemory_pc_kernel(
                         )
             nc.scalar.copy(
                 out=wsum_grouped[b][:, T_HALF * h : T_HALF * (h + 1)].rearrange(
-                    "p T r s t -> p (T r) s t"
-                )[:, :, c * PER_CHUNK : (c + 1) * PER_CHUNK, :],
-                in_=sums[:].rearrange("p T r s t -> p (T r) s t"),
+                    "p T r s t -> p T r (s t)"
+                )[:, :, :, c * PER_CHUNK * PACK : (c + 1) * PER_CHUNK * PACK],
+                in_=sums[:, :, 0:ROW_GROUPS].rearrange("p T r s t -> p T r (s t)"),
             )
 
         def quantise_bank_sums(b, h):
@@ -196,6 +200,13 @@ def tile_proceduralmemory_pc_kernel(
                     "p T r s t -> p (T r s t)"
                 ),
             )
+
+        def keep_warm(count):
+            for k in range(count):
+                unread = psum_post.tile([P, HALF], F32, tag="post")
+                nc.tensor.matmul(
+                    out=unread[:], lhsT=ones[:], rhs=zeros[:], start=True, stop=True
+                )
 
         def spread_bias():
             for h in range(FEAT // HALF):
@@ -268,10 +279,13 @@ def tile_proceduralmemory_pc_kernel(
                 out=out[b].rearrange("(p nb) d -> p nb d", nb=BLOCKS)[:, nb, :], in_=result[:]
             )
 
+        keep_warm(3)
         quantise_tokens(0, 0)
-        quantise_tokens(0, 1)
         spread_bias()
+        quantise_tokens(0, 1)
+        keep_warm(1)
         quantise_tokens(1, 0)
+        keep_warm(1)
         quantise_tokens(1, 1)
         for c in range(CHUNKS):
             for h in range(PACK // T_HALF):

@@ -44,7 +44,7 @@ def tile_proceduralmemory_pc_kernel(
         consts = ctx.enter_context(tc.tile_pool(name="consts", bufs=1))
         sample = ctx.enter_context(tc.tile_pool(name="sample", bufs=SAMPLES))
         halves = ctx.enter_context(tc.tile_pool(name="halves", bufs=2 * SAMPLES))
-        banks = ctx.enter_context(tc.tile_pool(name="banks", bufs=SAMPLES * CHUNKS))
+        banks = ctx.enter_context(tc.tile_pool(name="banks", bufs=SAMPLES * (CHUNKS + 1)))
         work = ctx.enter_context(tc.tile_pool(name="work", bufs=4))
         results = ctx.enter_context(tc.tile_pool(name="results", bufs=SAMPLES * BLOCKS))
         psum_sums = ctx.enter_context(tc.psum_pool(name="psum_sums", bufs=2))
@@ -89,12 +89,21 @@ def tile_proceduralmemory_pc_kernel(
         def load_banks(b):
             rows_view = W_pm[b].rearrange("k (r s) j -> (k r) s j", s=ROWS)
             for c in range(CHUNKS):
-                chunk_tile = banks.tile([P, CHUNK_ROWS, MEM], BF16)
-                nc.sync.dma_start(
-                    out=chunk_tile[:],
-                    in_=rows_view[:, c * CHUNK_ROWS : (c + 1) * CHUNK_ROWS, :],
-                )
-                bank_rows[(b, c)] = chunk_tile
+                chunk_view = rows_view[:, c * CHUNK_ROWS : (c + 1) * CHUNK_ROWS, :]
+                split_view = chunk_view.rearrange("q (s T) j -> q s T j", T=PACK)
+                if c < CHUNKS - 1:
+                    chunk_tile = banks.tile([P, PER_CHUNK, PACK, MEM], BF16, tag="chunk")
+                    nc.sync.dma_start(
+                        out=chunk_tile[:].rearrange("q s T j -> q (s T) j"), in_=chunk_view
+                    )
+                for h in range(PACK // T_HALF):
+                    residues = slice(h * T_HALF, (h + 1) * T_HALF)
+                    if c < CHUNKS - 1:
+                        bank_rows[(b, c, h)] = chunk_tile[:, :, residues, :]
+                    else:
+                        half_tile = banks.tile([P, PER_CHUNK, T_HALF, MEM], BF16, tag="chunk")
+                        nc.sync.dma_start(out=half_tile[:], in_=split_view[:, :, residues, :])
+                        bank_rows[(b, c, h)] = half_tile[:]
 
         def load_bias():
             nc.sync.dma_start(
@@ -113,8 +122,8 @@ def tile_proceduralmemory_pc_kernel(
                 )
 
         load_tokens(0, 0)
-        load_tokens(0, 1)
         load_bias()
+        load_tokens(0, 1)
         load_tokens(1, 0)
         load_tokens(1, 1)
         load_banks(0)
@@ -140,7 +149,7 @@ def tile_proceduralmemory_pc_kernel(
             wsum_codes[b] = codes_w
             wsum_scales[b] = scales_w
 
-        def quantise_tokens(b, half):
+        def quantise_tokens(b, half, pool, tag, copies):
             words = pre_rows[(b, half)][:].rearrange("p nb j -> p (nb j)").bitcast(F32)
             grouped = halves.tile([P, HALF_BLOCKS, P, PACK], BF16, align_bytes=64)
             grouped_words = (
@@ -150,7 +159,7 @@ def tile_proceduralmemory_pc_kernel(
                 .rearrange("p (nb n u) -> p nb n u", nb=HALF_BLOCKS, u=WORD_PACK)
             )
             for pair in range(HALF_BLOCKS // PAIR):
-                flipped = psum_product.tile([P, PAIR, WORD_PACK, P], F32, tag="product")
+                flipped = pool.tile([P, PAIR, WORD_PACK, P], F32, tag=tag)
                 for k in range(PAIR):
                     row = (pair * PAIR + k) * WORDS
                     for u in range(WORD_PACK):
@@ -159,8 +168,7 @@ def tile_proceduralmemory_pc_kernel(
                             in_=words[:, row + u : row + WORDS : WORD_PACK],
                             identity=ident[:],
                         )
-                copy = nc.scalar.copy if pair % 2 == 0 else nc.vector.tensor_copy
-                copy(
+                copies[pair](
                     out=grouped_words[:, pair * PAIR : (pair + 1) * PAIR, :, :],
                     in_=flipped[:].rearrange("p k u n -> p k n u"),
                 )
@@ -175,11 +183,10 @@ def tile_proceduralmemory_pc_kernel(
             sums = psum_sums.tile([P, T_HALF, FOLD, PER_CHUNK, PACK], F32, tag="sums")
             for k in range(T_HALF):
                 for s1 in range(PER_CHUNK):
-                    s = PACK * s1 + T_HALF * h + k
                     for t in range(PACK):
                         nc.tensor.matmul(
                             out=sums[:, k, :, s1, t],
-                            lhsT=bank_rows[(b, c)][:, s, t:MEM:PACK],
+                            lhsT=bank_rows[(b, c, h)][:, s1, k, t:MEM:PACK],
                             rhs=fold[:],
                             start=True,
                             stop=True,
@@ -279,34 +286,35 @@ def tile_proceduralmemory_pc_kernel(
                 out=out[b].rearrange("(p nb) d -> p nb d", nb=BLOCKS)[:, nb, :], in_=result[:]
             )
 
+        both = [nc.scalar.copy, nc.vector.tensor_copy]
         keep_warm(3)
-        quantise_tokens(0, 0)
+        quantise_tokens(0, 0, psum_product, "product", both)
         spread_bias()
-        quantise_tokens(0, 1)
+        quantise_tokens(0, 1, psum_product, "product", both)
         keep_warm(1)
-        quantise_tokens(1, 0)
+        quantise_tokens(1, 0, psum_product, "product", both)
         keep_warm(1)
-        quantise_tokens(1, 1)
+        quantise_tokens(1, 1, psum_product, "product", both)
         for c in range(CHUNKS):
             for h in range(PACK // T_HALF):
                 sum_banks(0, c, h)
                 if c == CHUNKS - 1:
                     quantise_bank_sums(0, h)
 
-        sums_at = {-1: [0], 0: [1], 1: [2], 2: [3], 3: [4, 5], 4: [6, 7]}
+        chunk_at = {-2: 0, 0: 1, 2: 2, 3: 3}
         n_blocks = SAMPLES * BLOCKS
         for step in range(-3, n_blocks):
             if 0 <= step + 1 < n_blocks:
                 second_product(step + 1)
+            if step + 3 < n_blocks:
+                first_product(step + 3)
             if step >= 0:
                 add_bias_and_store(step)
             if 0 <= step + 2 < n_blocks:
                 quantise_post(step + 2)
-            for k in sums_at.get(step, []):
-                c, h = divmod(k, PACK // T_HALF)
-                sum_banks(1, c, h)
-            if step + 3 == BLOCKS:
+            if step in chunk_at:
+                for h in range(PACK // T_HALF):
+                    sum_banks(1, chunk_at[step], h)
+            if step + 4 == BLOCKS:
                 for h in range(PACK // T_HALF):
                     quantise_bank_sums(1, h)
-            if step + 3 < n_blocks:
-                first_product(step + 3)

@@ -122,14 +122,15 @@ def tile_proceduralmemory_pc_kernel(
                 )
 
         load_tokens(0, 0)
-        load_bias()
         load_tokens(0, 1)
+        load_bias()
         load_tokens(1, 0)
-        load_tokens(1, 1)
         load_banks(0)
         load_projection()
+        load_tokens(1, 1)
         load_banks(1)
 
+        pre_grouped = {}
         pre_codes = {}
         pre_scales = {}
         wsum_grouped = {}
@@ -149,7 +150,7 @@ def tile_proceduralmemory_pc_kernel(
             wsum_codes[b] = codes_w
             wsum_scales[b] = scales_w
 
-        def quantise_tokens(b, half, pool, tag, copies):
+        def transpose_tokens(b, half, pool, tag, copies):
             words = pre_rows[(b, half)][:].rearrange("p nb j -> p (nb j)").bitcast(F32)
             grouped = halves.tile([P, HALF_BLOCKS, P, PACK], BF16, align_bytes=64)
             grouped_words = (
@@ -172,11 +173,14 @@ def tile_proceduralmemory_pc_kernel(
                     out=grouped_words[:, pair * PAIR : (pair + 1) * PAIR, :, :],
                     in_=flipped[:].rearrange("p k u n -> p k n u"),
                 )
+            pre_grouped[(b, half)] = grouped
+
+        def quantise_tokens(b, half):
             cols = slice(half * HALF_BLOCKS * P, (half + 1) * HALF_BLOCKS * P)
             nc.vector.quantize_mx(
                 out=pre_codes[b][:, cols].bitcast(FP8X4),
                 scales=pre_scales[b][:, cols],
-                in_=grouped[:].rearrange("p nb n t -> p (nb n t)"),
+                in_=pre_grouped[(b, half)][:].rearrange("p nb n t -> p (nb n t)"),
             )
 
         def sum_banks(b, c, h):
@@ -276,32 +280,37 @@ def tile_proceduralmemory_pc_kernel(
 
         def add_bias_and_store(g):
             b, nb = divmod(g, BLOCKS)
+            out_rows = out[b].rearrange("(p nb) d -> p nb d", nb=BLOCKS)[:, nb, :]
             result = results.tile([P, FEAT], F32)
             for h in range(FEAT // HALF):
                 cols = slice(h * HALF, (h + 1) * HALF)
                 nc.vector.tensor_tensor(
                     out=result[:, cols], in0=products[(g, h)][:], in1=bias_all[:, cols], op=ADD
                 )
-            nc.sync.dma_start(
-                out=out[b].rearrange("(p nb) d -> p nb d", nb=BLOCKS)[:, nb, :], in_=result[:]
-            )
+                if g == SAMPLES * BLOCKS - 1:
+                    nc.sync.dma_start(out=out_rows[:, cols], in_=result[:, cols])
+            if g < SAMPLES * BLOCKS - 1:
+                nc.sync.dma_start(out=out_rows, in_=result[:])
 
         both = [nc.scalar.copy, nc.vector.tensor_copy]
+        scalar_only = [nc.scalar.copy, nc.scalar.copy]
         keep_warm(3)
-        quantise_tokens(0, 0, psum_product, "product", both)
+        transpose_tokens(0, 0, psum_product, "product", both)
+        quantise_tokens(0, 0)
         spread_bias()
-        quantise_tokens(0, 1, psum_product, "product", both)
+        transpose_tokens(0, 1, psum_product, "product", both)
+        quantise_tokens(0, 1)
         keep_warm(1)
-        quantise_tokens(1, 0, psum_product, "product", both)
+        transpose_tokens(1, 0, psum_product, "product", both)
+        quantise_tokens(1, 0)
         keep_warm(1)
-        quantise_tokens(1, 1, psum_product, "product", both)
         for c in range(CHUNKS):
             for h in range(PACK // T_HALF):
                 sum_banks(0, c, h)
                 if c == CHUNKS - 1:
                     quantise_bank_sums(0, h)
 
-        chunk_at = {-2: 0, 0: 1, 2: 2, 3: 3}
+        chunk_at = {-1: 0, 0: 1, 2: 2, 3: 3}
         n_blocks = SAMPLES * BLOCKS
         for step in range(-3, n_blocks):
             if 0 <= step + 1 < n_blocks:
@@ -312,6 +321,10 @@ def tile_proceduralmemory_pc_kernel(
                 add_bias_and_store(step)
             if 0 <= step + 2 < n_blocks:
                 quantise_post(step + 2)
+            if step == -3:
+                transpose_tokens(1, 1, psum_sums, "sums", scalar_only)
+            if step == 0:
+                quantise_tokens(1, 1)
             if step in chunk_at:
                 for h in range(PACK // T_HALF):
                     sum_banks(1, chunk_at[step], h)

from contextlib import ExitStack

import concourse.mybir as mybir
from concourse.masks import make_identity

FLOPS = 2 * 2 * 1024 * 512 * 512 + 2 * 2 * 1024 * 512 * 1024

FP8X4 = mybir.dt.float8_e4m3fn_x4
BF16 = mybir.dt.bfloat16
F32 = mybir.dt.float32
I32 = mybir.dt.int32
U32 = mybir.dt.uint32
U8 = mybir.dt.uint8
ADD = mybir.AluOpType.add

P = 128
PACK = 4
SAMPLES = 2
TOKENS = 1024
MEM = 512
FEAT = 1024
BANKS = 8
BLOCKS = TOKENS // P
HALF = 512
ROW_GROUPS = P // BANKS
FOLD = 24
ROWS = MEM // ROW_GROUPS
CHUNK_ROWS = 8
CHUNKS = ROWS // CHUNK_ROWS
PER_CHUNK = CHUNK_ROWS // PACK
T_HALF = PACK // 2
HALF_BLOCKS = BLOCKS // 2
PAIR = 2
WORDS = MEM // 2
WORD_PACK = PACK // 2


def tile_proceduralmemory_pc_kernel(
    tc, pre, W_pm, proj_out_w_words, proj_out_w_scales, proj_out_b, out
):
    nc = tc.nc
    with ExitStack() as ctx:
        ctx.enter_context(tc.manual_schedule())
        consts = ctx.enter_context(tc.tile_pool(name="consts", bufs=1))
        sample = ctx.enter_context(tc.tile_pool(name="sample", bufs=SAMPLES))
        halves = ctx.enter_context(tc.tile_pool(name="halves", bufs=2 * SAMPLES))
        banks = ctx.enter_context(tc.tile_pool(name="banks", bufs=SAMPLES * (CHUNKS + 1)))
        work = ctx.enter_context(tc.tile_pool(name="work", bufs=4))
        results = ctx.enter_context(tc.tile_pool(name="results", bufs=SAMPLES * BLOCKS))
        psum_sums = ctx.enter_context(tc.psum_pool(name="psum_sums", bufs=2))
        psum_post = ctx.enter_context(tc.psum_pool(name="psum_post", bufs=2))
        psum_product = ctx.enter_context(tc.psum_pool(name="psum_product", bufs=4))

        ident = consts.tile([P, P], F32)
        make_identity(nc, ident[:])
        ones = consts.tile([P, P], BF16)
        nc.vector.memset(ones[:], 1.0)
        bias_row = consts.tile([P, FEAT], BF16)
        nc.vector.memset(bias_row[:], 0.0)
        bias_all = consts.tile([P, FEAT], F32)
        zeros = consts.tile([P, HALF], BF16)
        nc.vector.memset(zeros[:], 0.0)
        w_words = consts.tile([P, FEAT], U32, align_bytes=64)
        w_scales = consts.tile([P, FEAT], U8, align_bytes=64)
        nc.vector.memset(w_scales[:].bitcast(I32), 0)
        fold_f32 = consts.tile([P, ROW_GROUPS], F32)
        nc.vector.tensor_reduce(
            out=fold_f32[:],
            in_=ident[:].rearrange("q (k r) -> q r k", r=ROW_GROUPS),
            axis=mybir.AxisListType.X,
            op=ADD,
        )
        fold = consts.tile([P, FOLD], BF16)
        nc.vector.memset(fold[:], 0.0)
        nc.vector.tensor_copy(out=fold[:, 0:ROW_GROUPS], in_=fold_f32[:])

        pre_rows = {}
        bank_rows = {}

        def load_tokens(b, half):
            tokens_view = pre[b].rearrange("(p nb) j -> p nb j", nb=BLOCKS)
            pre_tile = halves.tile([P, HALF_BLOCKS, MEM], BF16)
            nc.sync.dma_start(
                out=pre_tile[:],
                in_=tokens_view[:, half * HALF_BLOCKS : (half + 1) * HALF_BLOCKS, :],
            )
            pre_rows[(b, half)] = pre_tile

        def load_banks(b):
            rows_view = W_pm[b].rearrange("k (r s) j -> (k r) s j", s=ROWS)
            for c in range(CHUNKS):
                chunk_view = rows_view[:, c * CHUNK_ROWS : (c + 1) * CHUNK_ROWS, :]
                split_view = chunk_view.rearrange("q (s T) j -> q s T j", T=PACK)
                if c < CHUNKS - 1:
                    chunk_tile = banks.tile([P, PER_CHUNK, PACK, MEM], BF16, tag="chunk")
                    nc.sync.dma_start(
                        out=chunk_tile[:].rearrange("q s T j -> q (s T) j"), in_=chunk_view
                    )
                for h in range(PACK // T_HALF):
                    residues = slice(h * T_HALF, (h + 1) * T_HALF)
                    if c < CHUNKS - 1:
                        bank_rows[(b, c, h)] = chunk_tile[:, :, residues, :]
                    else:
                        half_tile = banks.tile([P, PER_CHUNK, T_HALF, MEM], BF16, tag="chunk")
                        nc.sync.dma_start(out=half_tile[:], in_=split_view[:, :, residues, :])
                        bank_rows[(b, c, h)] = half_tile[:]

        def load_bias():
            nc.sync.dma_start(
                out=bias_row[0:1, :], in_=proj_out_b.rearrange("(o d) -> o d", o=1)
            )

        def load_projection():
            nc.sync.dma_start(
                out=w_words[:].bitcast(I32),
                in_=proj_out_w_words[0].rearrange("p n t -> p (n t)").bitcast(I32),
            )
            for quadrant in range(4):
                nc.sync.dma_start(
                    out=w_scales[32 * quadrant : 32 * quadrant + 4, :].bitcast(I32),
                    in_=proj_out_w_scales[0, 4 * quadrant : 4 * quadrant + 4, :].bitcast(I32),
                )

        load_tokens(0, 0)
        load_tokens(0, 1)
        load_bias()
        load_tokens(1, 0)
        load_banks(0)
        load_projection()
        load_tokens(1, 1)
        load_banks(1)

        pre_grouped = {}
        pre_codes = {}
        pre_scales = {}
        wsum_grouped = {}
        wsum_codes = {}
        wsum_scales = {}
        for b in range(SAMPLES):
            codes = sample.tile([P, TOKENS], U32, align_bytes=64)
            scales = sample.tile([P, TOKENS], U8, align_bytes=64)
            grouped_sums = sample.tile(
                [P, PACK, ROW_GROUPS, ROWS // PACK, PACK], BF16, align_bytes=64
            )
            codes_w = sample.tile([P, MEM], U32, align_bytes=64)
            scales_w = sample.tile([P, MEM], U8, align_bytes=64)
            pre_codes[b] = codes
            pre_scales[b] = scales
            wsum_grouped[b] = grouped_sums
            wsum_codes[b] = codes_w
            wsum_scales[b] = scales_w

        def transpose_tokens(b, half, pool, tag, copies):
            words = pre_rows[(b, half)][:].rearrange("p nb j -> p (nb j)").bitcast(F32)
            grouped = halves.tile([P, HALF_BLOCKS, P, PACK], BF16, align_bytes=64)
            grouped_words = (
                grouped[:]
                .rearrange("p nb n t -> p (nb n t)")
                .bitcast(F32)
                .rearrange("p (nb n u) -> p nb n u", nb=HALF_BLOCKS, u=WORD_PACK)
            )
            for pair in range(HALF_BLOCKS // PAIR):
                flipped = pool.tile([P, PAIR, WORD_PACK, P], F32, tag=tag)
                for k in range(PAIR):
                    row = (pair * PAIR + k) * WORDS
                    for u in range(WORD_PACK):
                        nc.tensor.transpose(
                            out=flipped[:, k, u, :],
                            in_=words[:, row + u : row + WORDS : WORD_PACK],
                            identity=ident[:],
                        )
                copies[pair](
                    out=grouped_words[:, pair * PAIR : (pair + 1) * PAIR, :, :],
                    in_=flipped[:].rearrange("p k u n -> p k n u"),
                )
            pre_grouped[(b, half)] = grouped

        def quantise_tokens(b, half):
            cols = slice(half * HALF_BLOCKS * P, (half + 1) * HALF_BLOCKS * P)
            nc.vector.quantize_mx(
                out=pre_codes[b][:, cols].bitcast(FP8X4),
                scales=pre_scales[b][:, cols],
                in_=pre_grouped[(b, half)][:].rearrange("p nb n t -> p (nb n t)"),
            )

        def sum_banks(b, c, h):
            sums = psum_sums.tile([P, T_HALF, FOLD, PER_CHUNK, PACK], F32, tag="sums")
            for k in range(T_HALF):
                for s1 in range(PER_CHUNK):
                    for t in range(PACK):
                        nc.tensor.matmul(
                            out=sums[:, k, :, s1, t],
                            lhsT=bank_rows[(b, c, h)][:, s1, k, t:MEM:PACK],
                            rhs=fold[:],
                            start=True,
                            stop=True,
                        )
            nc.scalar.copy(
                out=wsum_grouped[b][:, T_HALF * h : T_HALF * (h + 1)].rearrange(
                    "p T r s t -> p T r (s t)"
                )[:, :, :, c * PER_CHUNK * PACK : (c + 1) * PER_CHUNK * PACK],
                in_=sums[:, :, 0:ROW_GROUPS].rearrange("p T r s t -> p T r (s t)"),
            )

        def quantise_bank_sums(b, h):
            cols = slice(h * T_HALF * P, (h + 1) * T_HALF * P)
            nc.vector.quantize_mx(
                out=wsum_codes[b][:, cols].bitcast(FP8X4),
                scales=wsum_scales[b][:, cols],
                in_=wsum_grouped[b][:, T_HALF * h : T_HALF * (h + 1)].rearrange(
                    "p T r s t -> p (T r s t)"
                ),
            )

        def keep_warm(count):
            for k in range(count):
                unread = psum_post.tile([P, HALF], F32, tag="post")
                nc.tensor.matmul(
                    out=unread[:], lhsT=ones[:], rhs=zeros[:], start=True, stop=True
                )

        def spread_bias():
            for h in range(FEAT // HALF):
                cols = slice(h * HALF, (h + 1) * HALF)
                spread = psum_post.tile([P, HALF], F32, tag="post")
                nc.tensor.matmul(
                    out=spread[:], lhsT=ones[:], rhs=bias_row[:, cols], start=True, stop=True
                )
                nc.scalar.copy(out=bias_all[:, cols], in_=spread[:])

        post_grouped = {}
        post_codes = {}
        post_scales = {}
        products = {}

        def first_product(g):
            b, nb = divmod(g, BLOCKS)
            post = psum_post.tile([P, PACK, P], F32, tag="post")
            tokens = slice(nb * P, (nb + 1) * P)
            for T in range(PACK):
                rows = slice(T * P, (T + 1) * P)
                nc.tensor.matmul_mx(
                    out=post[:, T, :],
                    lhsT=wsum_codes[b][:, rows].bitcast(FP8X4),
                    lhsT_scale=wsum_scales[b][:, rows],
                    rhs=pre_codes[b][:, tokens].bitcast(FP8X4),
                    rhs_scale=pre_scales[b][:, tokens],
                    start=True,
                    stop=True,
                )
            grouped_post = work.tile([P, P, PACK], BF16, align_bytes=64)
            nc.scalar.copy(out=grouped_post[:], in_=post[:].rearrange("p T n -> p n T"))
            post_grouped[g] = grouped_post

        def quantise_post(g):
            codes_p = work.tile([P, P], U32, align_bytes=64)
            scales_p = work.tile([P, P], U8, align_bytes=64)
            nc.vector.quantize_mx(
                out=codes_p[:].bitcast(FP8X4),
                scales=scales_p[:],
                in_=post_grouped[g][:].rearrange("p n T -> p (n T)"),
            )
            post_codes[g] = codes_p
            post_scales[g] = scales_p

        def second_product(g):
            for h in range(FEAT // HALF):
                cols = slice(h * HALF, (h + 1) * HALF)
                product = psum_product.tile([P, HALF], F32, tag="product")
                nc.tensor.matmul_mx(
                    out=product[:],
                    lhsT=post_codes[g][:].bitcast(FP8X4),
                    lhsT_scale=post_scales[g][:],
                    rhs=w_words[:, cols].bitcast(FP8X4),
                    rhs_scale=w_scales[:, cols],
                    start=True,
                    stop=True,
                )
                products[(g, h)] = product

        def add_bias_and_store(g):
            b, nb = divmod(g, BLOCKS)
            out_rows = out[b].rearrange("(p nb) d -> p nb d", nb=BLOCKS)[:, nb, :]
            result = results.tile([P, FEAT], F32)
            for h in range(FEAT // HALF):
                cols = slice(h * HALF, (h + 1) * HALF)
                nc.vector.tensor_tensor(
                    out=result[:, cols], in0=products[(g, h)][:], in1=bias_all[:, cols], op=ADD
                )
                if g == SAMPLES * BLOCKS - 1:
                    nc.sync.dma_start(out=out_rows[:, cols], in_=result[:, cols])
            if g < SAMPLES * BLOCKS - 1:
                nc.sync.dma_start(out=out_rows, in_=result[:])

        both = [nc.scalar.copy, nc.vector.tensor_copy]
        scalar_only = [nc.scalar.copy, nc.scalar.copy]
        keep_warm(3)
        transpose_tokens(0, 0, psum_product, "product", both)
        quantise_tokens(0, 0)
        spread_bias()
        transpose_tokens(0, 1, psum_product, "product", both)
        quantise_tokens(0, 1)
        keep_warm(1)
        transpose_tokens(1, 0, psum_product, "product", both)
        quantise_tokens(1, 0)
        keep_warm(1)
        for c in range(CHUNKS):
            for h in range(PACK // T_HALF):
                sum_banks(0, c, h)
                if c == CHUNKS - 1:
                    quantise_bank_sums(0, h)

        chunk_at = {-1: 0, 0: 1, 2: 2, 3: 3}
        n_blocks = SAMPLES * BLOCKS
        for step in range(-3, n_blocks):
            if 0 <= step + 1 < n_blocks:
                second_product(step + 1)
            if step + 3 < n_blocks:
                first_product(step + 3)
            if step >= 0:
                add_bias_and_store(step)
            if 0 <= step + 2 < n_blocks:
                quantise_post(step + 2)
            if step == -3:
                transpose_tokens(1, 1, psum_sums, "sums", scalar_only)
            if step == 0:
                quantise_tokens(1, 1)
            if step in chunk_at:
                for h in range(PACK // T_HALF):
                    sum_banks(1, chunk_at[step], h)
            if step + 4 == BLOCKS:
                for h in range(PACK // T_HALF):
                    quantise_bank_sums(1, h)
